import numpy as np
import ml_dtypes


def mxq(x, axis, fmt="e4m3"):
    dtype, down = {"e4m3": (ml_dtypes.float8_e4m3fn, 7), "e5m2": (ml_dtypes.float8_e5m2, 14)}[fmt]
    v = np.moveaxis(np.asarray(x, np.float32).astype(ml_dtypes.bfloat16).astype(np.float64), axis, -1)
    blocks = v.reshape(v.shape[:-1] + (-1, 32))
    amax = np.abs(blocks).max(-1, keepdims=True)
    byte = np.maximum(np.where(amax > 0, np.frexp(amax)[1] - 1 + 127, 0) - down, 1)
    scale = np.exp2(byte - 127.0)
    codes = (blocks / scale).astype(np.float32).astype(dtype).astype(np.float64)
    return np.moveaxis((codes * scale).reshape(v.shape), -1, axis)


WIDE = False


def mx_kscale(k):
    if not WIDE:
        return np.ones(k)
    levels = np.array([10, -10, 5, -5, 0])
    if k % 512:
        return np.exp2(np.random.permutation(np.resize(levels, k // 32))).repeat(32)
    a = np.empty((k // 512, 16))
    for p in range(k // 512):
        a[p, :8] = np.random.permutation(np.resize(levels, 8))
        for g in range(8):
            far = levels[np.abs(levels - a[p, g]) >= 10]
            a[p, g + 8] = far[np.random.randint(len(far))]
    return np.exp2(a.ravel()).repeat(32)


BF16 = ml_dtypes.bfloat16


def bf(x):
    return np.asarray(x, np.float32).astype(BF16)


def f64(x):
    return np.asarray(x).astype(np.float64)


B, S, E, H, F = 4, 1024, 512, 4, 4096
DH = E // H


def rms_norm(x):
    ms = np.mean(np.square(x), axis=2, keepdims=True)
    return x / np.sqrt(ms)


def setup_inputs():
    s = mx_kscale(E)
    c = 2.0 ** np.round(np.log2(np.sqrt(np.mean(np.square(s)))))
    r = (c / s)[:, None, None]
    row = 0.5 + 1.5 * np.random.random((B, S, 1))
    return {'x': bf(np.random.standard_normal((B, S, E)) * row * s[None, None, :]),
            'w_q': bf(np.random.standard_normal((E, H, DH)) * 1.5 / np.sqrt(E) * r),
            'w_k': bf(np.random.standard_normal((E, H, DH)) * 1.5 / np.sqrt(E) * r),
            'w_v': bf(np.random.standard_normal((E, H, DH)) / np.sqrt(E) * r)}


def reference(x, w_q, w_k, w_v):
    xq = mxq(rms_norm(f64(x)), 2, 'e4m3')
    q = (xq @ mxq(f64(w_q).reshape(E, H * DH), 0, 'e4m3')).reshape(B, S, H, DH)
    k = (xq @ mxq(f64(w_k).reshape(E, H * DH), 0, 'e4m3')).reshape(B, S, H, DH)
    v = (xq @ mxq(f64(w_v).reshape(E, H * DH), 0, 'e4m3')).reshape(B, S, H, DH)
    return q, k, v

@@ -1,0 +1,171 @@
+from contextlib import ExitStack
+
+import concourse.mybir as mybir
+from concourse.masks import make_identity
+
+BF16 = mybir.dt.bfloat16
+F32 = mybir.dt.float32
+U32 = mybir.dt.uint32
+U8 = mybir.dt.uint8
+FP8X4 = mybir.dt.float8_e4m3fn_x4
+ACT = mybir.ActivationFunctionType
+
+P = 128
+PACK = 4
+FEATURES = P * PACK
+HALVES = 2
+TOKENS = 4 * 1024
+TILES = TOKENS // P
+PAIR = 2
+GROUP = 4
+GROUPS = TILES // GROUP
+COLUMNS = 4 * 128
+PROJECTIONS = 3
+
+FLOPS = 2 * TOKENS * FEATURES * COLUMNS * PROJECTIONS
+
+
+def tile_encoder_pa_t_kernel(tc, x, w_q, w_k, w_v, out_0, out_1, out_2):
+    nc = tc.nc
+    x_tiles = x.rearrange("b (q j) e -> (b q) j e", j=TILES)
+    out_tiles = [
+        out.rearrange("b (q j) h d -> (b q) j (h d)", j=TILES)
+        for out in (out_0, out_1, out_2)
+    ]
+
+    with ExitStack() as ctx:
+        keep = ctx.enter_context(tc.tile_pool(name="keep", bufs=1))
+        x_pool = ctx.enter_context(tc.tile_pool(name="x", bufs=GROUPS))
+        w_pool = ctx.enter_context(tc.tile_pool(name="w", bufs=PROJECTIONS))
+        stat_pool = ctx.enter_context(tc.tile_pool(name="stat", bufs=6))
+        square_pool = ctx.enter_context(tc.tile_pool(name="square", bufs=4))
+        xn_pool = ctx.enter_context(tc.tile_pool(name="xn", bufs=6))
+        mx_pool = ctx.enter_context(tc.tile_pool(name="mx", bufs=6))
+        result_pool = ctx.enter_context(tc.tile_pool(name="result", bufs=4))
+        turned_pool = ctx.enter_context(tc.psum_pool(name="turned", bufs=2))
+        product_pool = ctx.enter_context(tc.psum_pool(name="product", bufs=6))
+
+        one = keep.tile([P, 1], F32)
+        nc.vector.memset(one[:], 1.0)
+        root_of_one = keep.tile([P, 1], F32)
+        nc.scalar.activation(out=root_of_one[:], in_=one[:], func=ACT.Sqrt)
+
+        x_groups = []
+        w_raws = []
+
+        def load_x(g):
+            x_group = x_pool.tile([P, GROUP, FEATURES], BF16)
+            nc.sync.dma_start(out=x_group[:], in_=x_tiles[:, g * GROUP : (g + 1) * GROUP, :])
+            x_groups.append(x_group)
+
+        load_x(0)
+        for w in (w_q, w_k, w_v):
+            w_raw = w_pool.tile([P, PACK, COLUMNS], BF16)
+            nc.sync.dma_start(
+                out=w_raw[:].rearrange("p t n -> p (t n)"),
+                in_=w.rearrange("(p t) h d -> p (t h d)", t=PACK),
+            )
+            w_raws.append(w_raw)
+        for g in range(1, GROUPS):
+            load_x(g)
+
+        identity = keep.tile([P, P], F32)
+        make_identity(nc, identity[:])
+
+        w_codes = []
+        w_scales = []
+
+        def prepare_weight(i):
+            w_grouped = w_pool.tile([P, COLUMNS, PACK], BF16, align_bytes=64)
+            nc.vector.tensor_copy(out=w_grouped[:], in_=w_raws[i][:].rearrange("p t n -> p n t"))
+            codes = w_pool.tile([P, COLUMNS], U32, align_bytes=64, name="w_codes")
+            scales = w_pool.tile([P, COLUMNS], U8, align_bytes=64, name="w_scales")
+            nc.vector.quantize_mx(
+                out=codes[:].bitcast(FP8X4),
+                scales=scales[:],
+                in_=w_grouped[:].rearrange("p n t -> p (n t)"),
+            )
+            w_codes.append(codes)
+            w_scales.append(scales)
+
+        def normalise(pair):
+            x_group = x_groups[pair * PAIR // GROUP]
+            first = pair * PAIR % GROUP
+            sum_squares = stat_pool.tile([P, PAIR], F32)
+            for j in range(PAIR):
+                squares = square_pool.tile([P, FEATURES], BF16)
+                nc.scalar.activation(
+                    out=squares[:],
+                    in_=x_group[:, first + j, :],
+                    func=ACT.Square,
+                    accum_out=sum_squares[:, j : j + 1],
+                )
+            rms = stat_pool.tile([P, PAIR], F32)
+            nc.scalar.activation(out=rms[:], in_=sum_squares[:], func=ACT.Sqrt, scale=1.0 / FEATURES)
+            inverse_rms = stat_pool.tile([P, PAIR], F32)
+            nc.vector.reciprocal(out=inverse_rms[:], in_=rms[:])
+            xn = xn_pool.tile([P, PAIR, FEATURES], BF16)
+            for j in range(PAIR):
+                nc.vector.tensor_scalar_mul(
+                    out=xn[:, j, :], in0=x_group[:, first + j, :], scalar1=inverse_rms[:, j : j + 1]
+                )
+            return xn
+
+        def turn_and_quantise(xn):
+            turned = turned_pool.tile([P, PAIR, HALVES, P], F32)
+            for j in range(PAIR):
+                words = xn[:, j, :].bitcast(F32)
+                for u in range(HALVES):
+                    nc.tensor.transpose(turned[:, j, u, :], words[:, u::HALVES], identity[:])
+            grouped = mx_pool.tile([P, PAIR, P, PACK], BF16, align_bytes=64)
+            nc.vector.tensor_copy(
+                out=grouped[:].bitcast(F32), in_=turned[:].rearrange("p j u r -> p j r u")
+            )
+            codes = mx_pool.tile([P, PAIR * P], U32, align_bytes=64)
+            scales = mx_pool.tile([P, PAIR * P], U8, align_bytes=64)
+            nc.vector.quantize_mx(
+                out=codes[:].bitcast(FP8X4),
+                scales=scales[:],
+                in_=grouped[:].rearrange("p j r t -> p (j r t)"),
+            )
+            return codes, scales
+
+        def project(g, i):
+            result = result_pool.tile([P, GROUP, COLUMNS], F32, tag="result%d" % i)
+            for j in range(GROUP):
+                codes, scales = quantised[(g * GROUP + j) // PAIR]
+                tokens = slice(j % PAIR * P, (j % PAIR + 1) * P)
+                product = product_pool.tile([P, COLUMNS], F32)
+                nc.tensor.matmul_mx(
+                    out=product[:],
+                    lhsT=codes[:, tokens].bitcast(FP8X4),
+                    lhsT_scale=scales[:, tokens],
+                    rhs=w_codes[i][:].bitcast(FP8X4),
+                    rhs_scale=w_scales[i][:],
+                    start=True,
+                    stop=True,
+                )
+                if j % 2 == 0:
+                    nc.scalar.copy(out=result[:, j, :], in_=product[:])
+                else:
+                    nc.vector.tensor_copy(out=result[:, j, :], in_=product[:])
+            nc.sync.dma_start(out=out_tiles[i][:, g * GROUP : (g + 1) * GROUP, :], in_=result[:])
+
+        pairs_in_group = GROUP // PAIR
+        xns = []
+        quantised = []
+        for pair in range(pairs_in_group):
+            xns.append(normalise(pair))
+            quantised.append(turn_and_quantise(xns[pair]))
+        for pair in range(pairs_in_group, 2 * pairs_in_group):
+            xns.append(normalise(pair))
+        for g in range(GROUPS):
+            for i in range(PROJECTIONS):
+                if g == 0:
+                    prepare_weight(i)
+                project(g, i)
+                if i < pairs_in_group and g + 1 < GROUPS:
+                    quantised.append(turn_and_quantise(xns[(g + 1) * pairs_in_group + i]))
+            if g + 2 < GROUPS:
+                for pair in range((g + 2) * pairs_in_group, (g + 3) * pairs_in_group):
+                    xns.append(normalise(pair))

@@ -35,9 +35,8 @@ def tile_encoder_pa_t_kernel(tc, x, w_q, w_k, w_v, out_0, out_1, out_2):
 
     with ExitStack() as ctx:
         keep = ctx.enter_context(tc.tile_pool(name="keep", bufs=1))
-        x_pool = ctx.enter_context(tc.tile_pool(name="x", bufs=GROUPS))
         w_pool = ctx.enter_context(tc.tile_pool(name="w", bufs=PROJECTIONS))
-        stat_pool = ctx.enter_context(tc.tile_pool(name="stat", bufs=6))
+        stat_pool = ctx.enter_context(tc.tile_pool(name="stat", bufs=4))
         square_pool = ctx.enter_context(tc.tile_pool(name="square", bufs=4))
         xn_pool = ctx.enter_context(tc.tile_pool(name="xn", bufs=6))
         mx_pool = ctx.enter_context(tc.tile_pool(name="mx", bufs=6))
@@ -45,127 +44,254 @@ def tile_encoder_pa_t_kernel(tc, x, w_q, w_k, w_v, out_0, out_1, out_2):
         turned_pool = ctx.enter_context(tc.psum_pool(name="turned", bufs=2))
         product_pool = ctx.enter_context(tc.psum_pool(name="product", bufs=6))
 
+        identity = keep.tile([P, P], F32)
+        make_identity(nc, identity[:])
+
+        ctx.enter_context(tc.manual_schedule())
+
         one = keep.tile([P, 1], F32)
         nc.vector.memset(one[:], 1.0)
         root_of_one = keep.tile([P, 1], F32)
         nc.scalar.activation(out=root_of_one[:], in_=one[:], func=ACT.Sqrt)
 
-        x_groups = []
+        x_all = keep.tile([P, TILES, FEATURES], BF16)
         w_raws = []
 
-        def load_x(g):
-            x_group = x_pool.tile([P, GROUP, FEATURES], BF16)
-            nc.sync.dma_start(out=x_group[:], in_=x_tiles[:, g * GROUP : (g + 1) * GROUP, :])
-            x_groups.append(x_group)
+        def load_x(first, count):
+            tiles = slice(first, first + count)
+            nc.sync.dma_start(out=x_all[:, tiles, :], in_=x_tiles[:, tiles, :])
 
-        load_x(0)
-        for w in (w_q, w_k, w_v):
+        def load_weight(w):
             w_raw = w_pool.tile([P, PACK, COLUMNS], BF16)
             nc.sync.dma_start(
                 out=w_raw[:].rearrange("p t n -> p (t n)"),
                 in_=w.rearrange("(p t) h d -> p (t h d)", t=PACK),
             )
             w_raws.append(w_raw)
+
+        load_x(0, PAIR)
+        load_weight(w_q)
+        load_x(PAIR, PAIR)
+        load_weight(w_k)
+        load_weight(w_v)
         for g in range(1, GROUPS):
-            load_x(g)
+            load_x(g * GROUP, GROUP)
 
-        identity = keep.tile([P, P], F32)
-        make_identity(nc, identity[:])
+        w_grouped = {}
+        w_codes = {}
+        w_scales = {}
 
-        w_codes = []
-        w_scales = []
+        def group_weight(i, copy):
+            w_grouped[i] = w_pool.tile([P, COLUMNS, PACK], BF16, align_bytes=64, name="w_grouped")
+            copy(out=w_grouped[i][:], in_=w_raws[i][:].rearrange("p t n -> p n t"))
 
-        def prepare_weight(i):
-            w_grouped = w_pool.tile([P, COLUMNS, PACK], BF16, align_bytes=64)
-            nc.vector.tensor_copy(out=w_grouped[:], in_=w_raws[i][:].rearrange("p t n -> p n t"))
-            codes = w_pool.tile([P, COLUMNS], U32, align_bytes=64, name="w_codes")
-            scales = w_pool.tile([P, COLUMNS], U8, align_bytes=64, name="w_scales")
+        def quantise_weight(i):
+            w_codes[i] = w_pool.tile([P, COLUMNS], U32, align_bytes=64, name="w_codes")
+            w_scales[i] = w_pool.tile([P, COLUMNS], U8, align_bytes=64, name="w_scales")
             nc.vector.quantize_mx(
-                out=codes[:].bitcast(FP8X4),
-                scales=scales[:],
-                in_=w_grouped[:].rearrange("p n t -> p (n t)"),
+                out=w_codes[i][:].bitcast(FP8X4),
+                scales=w_scales[i][:],
+                in_=w_grouped[i][:].rearrange("p n t -> p (n t)"),
             )
-            w_codes.append(codes)
-            w_scales.append(scales)
 
-        def normalise(pair):
-            x_group = x_groups[pair * PAIR // GROUP]
-            first = pair * PAIR % GROUP
-            sum_squares = stat_pool.tile([P, PAIR], F32)
-            for j in range(PAIR):
-                squares = square_pool.tile([P, FEATURES], BF16)
-                nc.scalar.activation(
-                    out=squares[:],
-                    in_=x_group[:, first + j, :],
-                    func=ACT.Square,
-                    accum_out=sum_squares[:, j : j + 1],
-                )
-            rms = stat_pool.tile([P, PAIR], F32)
-            nc.scalar.activation(out=rms[:], in_=sum_squares[:], func=ACT.Sqrt, scale=1.0 / FEATURES)
-            inverse_rms = stat_pool.tile([P, PAIR], F32)
-            nc.vector.reciprocal(out=inverse_rms[:], in_=rms[:])
-            xn = xn_pool.tile([P, PAIR, FEATURES], BF16)
-            for j in range(PAIR):
+        sum_squares = {}
+        rms = {}
+        xn = {}
+        turned = {}
+        grouped = {}
+        codes = {}
+        scales = {}
+
+        def sums(first, count):
+            block = stat_pool.tile([P, GROUP], F32, name="sum_squares")
+            for j in range(count):
+                sum_squares[first + j] = block[:, j : j + 1]
+            rms[first] = block[:, :count]
+
+        def square(tile):
+            squares = square_pool.tile([P, FEATURES], BF16)
+            nc.scalar.activation(
+                out=squares[:], in_=x_all[:, tile, :], func=ACT.Square, accum_out=sum_squares[tile]
+            )
+
+        def root(first, count):
+            roots = stat_pool.tile([P, GROUP], F32, name="rms")
+            nc.scalar.activation(
+                out=roots[:, :count], in_=rms[first], func=ACT.Sqrt, scale=1.0 / FEATURES
+            )
+            rms[first] = roots[:, :count]
+
+        def scale(first, count):
+            inverse_rms = stat_pool.tile([P, GROUP], F32)
+            nc.vector.reciprocal(out=inverse_rms[:, :count], in_=rms[first])
+            for j in range(count):
+                if j % PAIR == 0:
+                    pair_xn = xn_pool.tile([P, PAIR, FEATURES], BF16)
+                xn[first + j] = pair_xn[:, j % PAIR, :]
                 nc.vector.tensor_scalar_mul(
-                    out=xn[:, j, :], in0=x_group[:, first + j, :], scalar1=inverse_rms[:, j : j + 1]
+                    out=xn[first + j],
+                    in0=x_all[:, first + j, :],
+                    scalar1=inverse_rms[:, j : j + 1],
                 )
-            return xn
 
-        def turn_and_quantise(xn):
-            turned = turned_pool.tile([P, PAIR, HALVES, P], F32)
+        def turn(pair):
+            turned[pair] = turned_pool.tile([P, PAIR, HALVES, P], F32, name="turned")
             for j in range(PAIR):
-                words = xn[:, j, :].bitcast(F32)
+                words = xn[pair * PAIR + j].bitcast(F32)
                 for u in range(HALVES):
-                    nc.tensor.transpose(turned[:, j, u, :], words[:, u::HALVES], identity[:])
-            grouped = mx_pool.tile([P, PAIR, P, PACK], BF16, align_bytes=64)
+                    nc.tensor.transpose(turned[pair][:, j, u, :], words[:, u::HALVES], identity[:])
+
+        def group(pair):
+            grouped[pair] = mx_pool.tile([P, PAIR, P, PACK], BF16, align_bytes=64, name="grouped")
             nc.vector.tensor_copy(
-                out=grouped[:].bitcast(F32), in_=turned[:].rearrange("p j u r -> p j r u")
+                out=grouped[pair][:].bitcast(F32), in_=turned[pair][:].rearrange("p j u r -> p j r u")
             )
-            codes = mx_pool.tile([P, PAIR * P], U32, align_bytes=64)
-            scales = mx_pool.tile([P, PAIR * P], U8, align_bytes=64)
+
+        def quantise(pair):
+            codes[pair] = mx_pool.tile([P, PAIR * P], U32, align_bytes=64, name="codes")
+            scales[pair] = mx_pool.tile([P, PAIR * P], U8, align_bytes=64, name="scales")
             nc.vector.quantize_mx(
-                out=codes[:].bitcast(FP8X4),
-                scales=scales[:],
-                in_=grouped[:].rearrange("p j r t -> p (j r t)"),
+                out=codes[pair][:].bitcast(FP8X4),
+                scales=scales[pair][:],
+                in_=grouped[pair][:].rearrange("p j r t -> p (j r t)"),
             )
-            return codes, scales
 
-        def project(g, i):
-            result = result_pool.tile([P, GROUP, COLUMNS], F32, tag="result%d" % i)
-            for j in range(GROUP):
-                codes, scales = quantised[(g * GROUP + j) // PAIR]
-                tokens = slice(j % PAIR * P, (j % PAIR + 1) * P)
-                product = product_pool.tile([P, COLUMNS], F32)
-                nc.tensor.matmul_mx(
-                    out=product[:],
-                    lhsT=codes[:, tokens].bitcast(FP8X4),
-                    lhsT_scale=scales[:, tokens],
-                    rhs=w_codes[i][:].bitcast(FP8X4),
-                    rhs_scale=w_scales[i][:],
-                    start=True,
-                    stop=True,
+        products = {}
+        results = {}
+
+        def project(tile, i):
+            pair, j = divmod(tile, PAIR)
+            tokens = slice(j * P, (j + 1) * P)
+            products[tile, i] = product_pool.tile([P, COLUMNS], F32, name="product")
+            nc.tensor.matmul_mx(
+                out=products[tile, i][:],
+                lhsT=codes[pair][:, tokens].bitcast(FP8X4),
+                lhsT_scale=scales[pair][:, tokens],
+                rhs=w_codes[i][:].bitcast(FP8X4),
+                rhs_scale=w_scales[i][:],
+                start=True,
+                stop=True,
+            )
+
+        def empty(tile, i, copy):
+            g, j = divmod(tile, GROUP)
+            if j == 0:
+                results[i] = result_pool.tile(
+                    [P, GROUP, COLUMNS], F32, tag="result%d" % i, name="result"
                 )
-                if j % 2 == 0:
-                    nc.scalar.copy(out=result[:, j, :], in_=product[:])
-                else:
-                    nc.vector.tensor_copy(out=result[:, j, :], in_=product[:])
-            nc.sync.dma_start(out=out_tiles[i][:, g * GROUP : (g + 1) * GROUP, :], in_=result[:])
+            copy(out=results[i][:, j, :], in_=products[tile, i][:])
+            if j == GROUP - 1:
+                nc.sync.dma_start(
+                    out=out_tiles[i][:, g * GROUP : (g + 1) * GROUP, :], in_=results[i][:]
+                )
 
-        pairs_in_group = GROUP // PAIR
-        xns = []
-        quantised = []
-        for pair in range(pairs_in_group):
-            xns.append(normalise(pair))
-            quantised.append(turn_and_quantise(xns[pair]))
-        for pair in range(pairs_in_group, 2 * pairs_in_group):
-            xns.append(normalise(pair))
-        for g in range(GROUPS):
-            for i in range(PROJECTIONS):
-                if g == 0:
-                    prepare_weight(i)
-                project(g, i)
-                if i < pairs_in_group and g + 1 < GROUPS:
-                    quantised.append(turn_and_quantise(xns[(g + 1) * pairs_in_group + i]))
-            if g + 2 < GROUPS:
-                for pair in range((g + 2) * pairs_in_group, (g + 3) * pairs_in_group):
-                    xns.append(normalise(pair))
+        on_scalar = nc.scalar.copy
+        on_vector = nc.vector.tensor_copy
+
+        sums(0, PAIR)
+        square(0)
+        square(1)
+        root(0, PAIR)
+        scale(0, PAIR)
+        turn(0)
+        sums(PAIR, PAIR)
+        square(2)
+        square(3)
+        root(PAIR, PAIR)
+        group_weight(0, on_vector)
+        scale(PAIR, PAIR)
+        turn(1)
+        group(0)
+        quantise_weight(0)
+        quantise(0)
+        group_weight(1, on_scalar)
+        group(1)
+        quantise(1)
+        for j in range(GROUP):
+            project(j, 0)
+        quantise_weight(1)
+        empty(0, 0, on_scalar)
+        empty(1, 0, on_vector)
+        empty(2, 0, on_scalar)
+        empty(3, 0, on_vector)
+        for j in range(GROUP):
+            project(j, 1)
+        sums(GROUP, GROUP)
+        square(4)
+        square(5)
+        empty(0, 1, on_scalar)
+        empty(1, 1, on_vector)
+        square(6)
+        empty(2, 1, on_scalar)
+        empty(3, 1, on_vector)
+        square(7)
+        root(GROUP, GROUP)
+        group_weight(2, on_vector)
+        scale(GROUP, GROUP)
+        quantise_weight(2)
+        turn(2)
+        for j in range(GROUP):
+            project(j, 2)
+        turn(3)
+        group(2)
+        sums(2 * GROUP, GROUP)
+        square(8)
+        empty(0, 2, on_scalar)
+        empty(1, 2, on_vector)
+        quantise(2)
+        square(9)
+        empty(2, 2, on_scalar)
+        empty(3, 2, on_vector)
+        group(3)
+        square(10)
+        square(11)
+        root(2 * GROUP, GROUP)
+        scale(2 * GROUP, GROUP)
+        quantise(3)
+
+        for g in range(1, GROUPS):
+            a = g * GROUP
+            turned_pairs = range((g + 1) * GROUP // PAIR, (g + 2) * GROUP // PAIR) if g + 1 < GROUPS else []
+            norm = (g + 2) * GROUP if g + 2 < GROUPS else None
+
+            if norm is not None:
+                sums(norm, GROUP)
+            for j in range(GROUP):
+                project(a + j, 0)
+            empty(a, 0, on_scalar)
+            if norm is not None:
+                square(norm)
+            empty(a + 1, 0, on_vector)
+            empty(a + 2, 0, on_scalar)
+            if norm is not None:
+                square(norm + 1)
+            empty(a + 3, 0, on_vector)
+            for pair in turned_pairs[:1]:
+                turn(pair)
+                group(pair)
+            for j in range(GROUP):
+                project(a + j, 1)
+            empty(a, 1, on_scalar)
+            if norm is not None:
+                square(norm + 2)
+            empty(a + 1, 1, on_vector)
+            for pair in turned_pairs[:1]:
+                quantise(pair)
+            empty(a + 2, 1, on_scalar)
+            if norm is not None:
+                square(norm + 3)
+                root(norm, GROUP)
+            empty(a + 3, 1, on_vector)
+            for pair in turned_pairs[1:]:
+                turn(pair)
+                group(pair)
+            for j in range(GROUP):
+                project(a + j, 2)
+            empty(a, 2, on_scalar)
+            empty(a + 1, 2, on_vector)
+            for pair in turned_pairs[1:]:
+                quantise(pair)
+            empty(a + 2, 2, on_scalar)
+            empty(a + 3, 2, on_vector)
+            if norm is not None:
+                scale(norm, GROUP)

@@ -209,45 +209,40 @@ def tile_encoder_pa_t_kernel(tc, x, w_q, w_k, w_v, out_0, out_1, out_2):
         quantise(1)
         for j in range(GROUP):
             project(j, 0)
+        sums(GROUP, GROUP)
+        for j in range(GROUP):
+            square(GROUP + j)
+        root(GROUP, GROUP)
         quantise_weight(1)
-        empty(0, 0, on_scalar)
+        empty(0, 0, on_vector)
         empty(1, 0, on_vector)
         empty(2, 0, on_scalar)
-        empty(3, 0, on_vector)
+        empty(3, 0, on_scalar)
         for j in range(GROUP):
             project(j, 1)
-        sums(GROUP, GROUP)
-        square(4)
-        square(5)
-        empty(0, 1, on_scalar)
-        empty(1, 1, on_vector)
-        square(6)
-        empty(2, 1, on_scalar)
-        empty(3, 1, on_vector)
-        square(7)
-        root(GROUP, GROUP)
-        group_weight(2, on_vector)
         scale(GROUP, GROUP)
-        quantise_weight(2)
         turn(2)
-        for j in range(GROUP):
-            project(j, 2)
         turn(3)
+        group_weight(2, on_vector)
+        for j in range(GROUP):
+            empty(j, 1, on_scalar)
         group(2)
+        quantise_weight(2)
+        group(3)
+        quantise(2)
+        quantise(3)
         sums(2 * GROUP, GROUP)
         square(8)
-        empty(0, 2, on_scalar)
-        empty(1, 2, on_vector)
-        quantise(2)
         square(9)
-        empty(2, 2, on_scalar)
-        empty(3, 2, on_vector)
-        group(3)
+        for j in range(GROUP):
+            project(j, 2)
+        empty(0, 2, on_scalar)
         square(10)
+        empty(1, 2, on_vector)
+        empty(2, 2, on_scalar)
         square(11)
         root(2 * GROUP, GROUP)
-        scale(2 * GROUP, GROUP)
-        quantise(3)
+        empty(3, 2, on_vector)
 
         for g in range(1, GROUPS):
             a = g * GROUP
@@ -266,27 +261,29 @@ def tile_encoder_pa_t_kernel(tc, x, w_q, w_k, w_v, out_0, out_1, out_2):
             if norm is not None:
                 square(norm + 1)
             empty(a + 3, 0, on_vector)
-            for pair in turned_pairs[:1]:
-                turn(pair)
-                group(pair)
+            if g == 1:
+                scale(2 * GROUP, GROUP)
             for j in range(GROUP):
                 project(a + j, 1)
+            for pair in turned_pairs:
+                turn(pair)
+            for j in range(GROUP):
+                project(a + j, 2)
             empty(a, 1, on_scalar)
             if norm is not None:
                 square(norm + 2)
             empty(a + 1, 1, on_vector)
             for pair in turned_pairs[:1]:
-                quantise(pair)
+                group(pair)
             empty(a + 2, 1, on_scalar)
             if norm is not None:
                 square(norm + 3)
                 root(norm, GROUP)
             empty(a + 3, 1, on_vector)
             for pair in turned_pairs[1:]:
-                turn(pair)
                 group(pair)
-            for j in range(GROUP):
-                project(a + j, 2)
+            for pair in turned_pairs[:1]:
+                quantise(pair)
             empty(a, 2, on_scalar)
             empty(a + 1, 2, on_vector)
             for pair in turned_pairs[1:]:

@@ -9,6 +9,7 @@ U32 = mybir.dt.uint32
 U8 = mybir.dt.uint8
 FP8X4 = mybir.dt.float8_e4m3fn_x4
 ACT = mybir.ActivationFunctionType
+ALU = mybir.AluOpType
 
 P = 128
 PACK = 4
@@ -52,7 +53,7 @@ def tile_encoder_pa_t_kernel(tc, x, w_q, w_k, w_v, out_0, out_1, out_2):
         one = keep.tile([P, 1], F32)
         nc.vector.memset(one[:], 1.0)
         root_of_one = keep.tile([P, 1], F32)
-        nc.scalar.activation(out=root_of_one[:], in_=one[:], func=ACT.Sqrt)
+        nc.scalar.activation(out=root_of_one[:], in_=one[:], func=ACT.Abs_reciprocal_sqrt)
 
         x_all = keep.tile([P, TILES, FEATURES], BF16)
         w_raws = []
@@ -70,11 +71,12 @@ def tile_encoder_pa_t_kernel(tc, x, w_q, w_k, w_v, out_0, out_1, out_2):
             w_raws.append(w_raw)
 
         load_x(0, PAIR)
-        load_weight(w_q)
         load_x(PAIR, PAIR)
+        load_weight(w_q)
+        load_x(GROUP, GROUP)
         load_weight(w_k)
         load_weight(w_v)
-        for g in range(1, GROUPS):
+        for g in range(2, GROUPS):
             load_x(g * GROUP, GROUP)
 
         w_grouped = {}
@@ -95,7 +97,7 @@ def tile_encoder_pa_t_kernel(tc, x, w_q, w_k, w_v, out_0, out_1, out_2):
             )
 
         sum_squares = {}
-        rms = {}
+        inverse_rms = {}
         xn = {}
         turned = {}
         grouped = {}
@@ -106,7 +108,7 @@ def tile_encoder_pa_t_kernel(tc, x, w_q, w_k, w_v, out_0, out_1, out_2):
             block = stat_pool.tile([P, GROUP], F32, name="sum_squares")
             for j in range(count):
                 sum_squares[first + j] = block[:, j : j + 1]
-            rms[first] = block[:, :count]
+            inverse_rms[first] = block[:, :count]
 
         def square(tile):
             squares = square_pool.tile([P, FEATURES], BF16)
@@ -114,16 +116,29 @@ def tile_encoder_pa_t_kernel(tc, x, w_q, w_k, w_v, out_0, out_1, out_2):
                 out=squares[:], in_=x_all[:, tile, :], func=ACT.Square, accum_out=sum_squares[tile]
             )
 
-        def root(first, count):
-            roots = stat_pool.tile([P, GROUP], F32, name="rms")
-            nc.scalar.activation(
-                out=roots[:, :count], in_=rms[first], func=ACT.Sqrt, scale=1.0 / FEATURES
+        def square_on_vector(tile):
+            squares = square_pool.tile([P, FEATURES], BF16)
+            nc.vector.scalar_tensor_tensor(
+                out=squares[:],
+                in0=x_all[:, tile, :],
+                scalar=1.0,
+                in1=x_all[:, tile, :],
+                op0=ALU.mult,
+                op1=ALU.mult,
+                accum_out=sum_squares[tile],
             )
-            rms[first] = roots[:, :count]
+
+        def root(first, count):
+            roots = stat_pool.tile([P, GROUP], F32, name="inverse_rms")
+            nc.scalar.activation(
+                out=roots[:, :count],
+                in_=inverse_rms[first],
+                func=ACT.Abs_reciprocal_sqrt,
+                scale=1.0 / FEATURES,
+            )
+            inverse_rms[first] = roots[:, :count]
 
         def scale(first, count):
-            inverse_rms = stat_pool.tile([P, GROUP], F32)
-            nc.vector.reciprocal(out=inverse_rms[:, :count], in_=rms[first])
             for j in range(count):
                 if j % PAIR == 0:
                     pair_xn = xn_pool.tile([P, PAIR, FEATURES], BF16)
@@ -131,7 +146,7 @@ def tile_encoder_pa_t_kernel(tc, x, w_q, w_k, w_v, out_0, out_1, out_2):
                 nc.vector.tensor_scalar_mul(
                     out=xn[first + j],
                     in0=x_all[:, first + j, :],
-                    scalar1=inverse_rms[:, j : j + 1],
+                    scalar1=inverse_rms[first][:, j : j + 1],
                 )
 
         def turn(pair):
@@ -141,9 +156,9 @@ def tile_encoder_pa_t_kernel(tc, x, w_q, w_k, w_v, out_0, out_1, out_2):
                 for u in range(HALVES):
                     nc.tensor.transpose(turned[pair][:, j, u, :], words[:, u::HALVES], identity[:])
 
-        def group(pair):
+        def group(pair, copy):
             grouped[pair] = mx_pool.tile([P, PAIR, P, PACK], BF16, align_bytes=64, name="grouped")
-            nc.vector.tensor_copy(
+            copy(
                 out=grouped[pair][:].bitcast(F32), in_=turned[pair][:].rearrange("p j u r -> p j r u")
             )
 
@@ -188,107 +203,119 @@ def tile_encoder_pa_t_kernel(tc, x, w_q, w_k, w_v, out_0, out_1, out_2):
         on_scalar = nc.scalar.copy
         on_vector = nc.vector.tensor_copy
 
+        def step(g, now, ahead):
+            a = g * GROUP
+            b = a + GROUP
+            pairs = [b // PAIR, b // PAIR + 1]
+            more = g + 1 < GROUPS
+            if ahead and ahead[0] == b + GROUP:
+                sums(b + GROUP, GROUP)
+            now = list(now)
+            ahead = list(ahead)
+            for i in (0, 1):
+                for j in range(GROUP):
+                    project(a + j, i)
+            empty(a, 0, on_scalar)
+            empty(a + 1, 0, on_vector)
+            for tile in now[:1]:
+                square(tile)
+            empty(a + 2, 0, on_scalar)
+            empty(a + 3, 0, on_vector)
+            for tile in now[1:]:
+                square(tile)
+            if now:
+                root(b, GROUP)
+            empty(a, 1, on_scalar)
+            empty(a + 1, 1, on_vector)
+            if more:
+                scale(b, GROUP)
+                for pair in pairs:
+                    turn(pair)
+            for j in range(GROUP):
+                project(a + j, 2)
+            empty(a + 2, 1, on_scalar)
+            empty(a + 3, 1, on_vector)
+            for tile in ahead[:2]:
+                square(tile)
+            if more:
+                group(pairs[0], on_vector)
+                group(pairs[1], on_vector)
+                quantise(pairs[0])
+            empty(a, 2, on_scalar)
+            empty(a + 1, 2, on_vector)
+            for tile in ahead[2:3]:
+                square(tile)
+            if more:
+                quantise(pairs[1])
+            empty(a + 2, 2, on_scalar)
+            empty(a + 3, 2, on_vector)
+            for tile in ahead[3:]:
+                square(tile)
+            if len(ahead) > 0 and ahead[-1] == b + 2 * GROUP - 1:
+                root(b + GROUP, GROUP)
+
+
         sums(0, PAIR)
         square(0)
-        square(1)
+        square_on_vector(1)
         root(0, PAIR)
-        scale(0, PAIR)
-        turn(0)
         sums(PAIR, PAIR)
         square(2)
-        square(3)
+        square_on_vector(3)
         root(PAIR, PAIR)
+        scale(0, PAIR)
+        turn(0)
         group_weight(0, on_vector)
         scale(PAIR, PAIR)
         turn(1)
-        group(0)
+        sums(GROUP, GROUP)
+        group(0, on_scalar)
+        square(4)
         quantise_weight(0)
         quantise(0)
-        group_weight(1, on_scalar)
-        group(1)
+        group(1, on_scalar)
+        group_weight(1, on_vector)
         quantise(1)
         for j in range(GROUP):
             project(j, 0)
-        sums(GROUP, GROUP)
-        for j in range(GROUP):
-            square(GROUP + j)
-        root(GROUP, GROUP)
+        square(5)
         quantise_weight(1)
-        empty(0, 0, on_vector)
+        empty(0, 0, on_scalar)
         empty(1, 0, on_vector)
+        square(6)
         empty(2, 0, on_scalar)
-        empty(3, 0, on_scalar)
+        empty(3, 0, on_vector)
+        square(7)
+        root(GROUP, GROUP)
         for j in range(GROUP):
             project(j, 1)
+        group_weight(2, on_vector)
+        empty(0, 1, on_scalar)
         scale(GROUP, GROUP)
         turn(2)
         turn(3)
-        group_weight(2, on_vector)
-        for j in range(GROUP):
-            empty(j, 1, on_scalar)
-        group(2)
+        empty(1, 1, on_scalar)
+        empty(2, 1, on_scalar)
         quantise_weight(2)
-        group(3)
-        quantise(2)
-        quantise(3)
-        sums(2 * GROUP, GROUP)
-        square(8)
-        square(9)
+        empty(3, 1, on_vector)
         for j in range(GROUP):
             project(j, 2)
+        sums(8, GROUP)
+        square(8)
+        square(9)
+        group(2, on_vector)
+        group(3, on_vector)
+        quantise(2)
         empty(0, 2, on_scalar)
-        square(10)
         empty(1, 2, on_vector)
+        quantise(3)
+        square_on_vector(11)
         empty(2, 2, on_scalar)
-        square(11)
-        root(2 * GROUP, GROUP)
-        empty(3, 2, on_vector)
-
-        for g in range(1, GROUPS):
-            a = g * GROUP
-            turned_pairs = range((g + 1) * GROUP // PAIR, (g + 2) * GROUP // PAIR) if g + 1 < GROUPS else []
-            norm = (g + 2) * GROUP if g + 2 < GROUPS else None
-
-            if norm is not None:
-                sums(norm, GROUP)
-            for j in range(GROUP):
-                project(a + j, 0)
-            empty(a, 0, on_scalar)
-            if norm is not None:
-                square(norm)
-            empty(a + 1, 0, on_vector)
-            empty(a + 2, 0, on_scalar)
-            if norm is not None:
-                square(norm + 1)
-            empty(a + 3, 0, on_vector)
-            if g == 1:
-                scale(2 * GROUP, GROUP)
-            for j in range(GROUP):
-                project(a + j, 1)
-            for pair in turned_pairs:
-                turn(pair)
-            for j in range(GROUP):
-                project(a + j, 2)
-            empty(a, 1, on_scalar)
-            if norm is not None:
-                square(norm + 2)
-            empty(a + 1, 1, on_vector)
-            for pair in turned_pairs[:1]:
-                group(pair)
-            empty(a + 2, 1, on_scalar)
-            if norm is not None:
-                square(norm + 3)
-                root(norm, GROUP)
-            empty(a + 3, 1, on_vector)
-            for pair in turned_pairs[1:]:
-                group(pair)
-            for pair in turned_pairs[:1]:
-                quantise(pair)
-            empty(a, 2, on_scalar)
-            empty(a + 1, 2, on_vector)
-            for pair in turned_pairs[1:]:
-                quantise(pair)
-            empty(a + 2, 2, on_scalar)
-            empty(a + 3, 2, on_vector)
-            if norm is not None:
-                scale(norm, GROUP)
+        empty(3, 2, on_scalar)
+        step(1, [10], [12,13,14])
+        step(2, [15], [16,17,18,19])
+        step(3, [], [20,21,22,23])
+        step(4, [], [24,25,26,27])
+        step(5, [], [28,29,30,31])
+        step(6, [], [])
+        step(7, [], [])

@@ -76,8 +76,16 @@ def tile_encoder_pa_t_kernel(tc, x, w_q, w_k, w_v, out_0, out_1, out_2):
         load_x(GROUP, GROUP)
         load_weight(w_k)
         load_weight(w_v)
-        for g in range(2, GROUPS):
-            load_x(g * GROUP, GROUP)
+        load_x(2 * GROUP, 2 * GROUP)
+        load_x(4 * GROUP, 4 * GROUP)
+
+        zeros = keep.tile([P, COLUMNS], BF16)
+        nc.vector.memset(zeros[:], 0.0)
+        warm = product_pool.tile([P, COLUMNS], F32, name="product")
+
+        def warm_up(count):
+            for _ in range(count):
+                nc.tensor.matmul(out=warm[:], lhsT=zeros[:, :P], rhs=zeros[:], start=True, stop=True)
 
         w_grouped = {}
         w_codes = {}
@@ -255,6 +263,7 @@ def tile_encoder_pa_t_kernel(tc, x, w_q, w_k, w_v, out_0, out_1, out_2):
                 root(b + GROUP, GROUP)
 
 
+        warm_up(6)
         sums(0, PAIR)
         square(0)
         square_on_vector(1)
@@ -265,9 +274,11 @@ def tile_encoder_pa_t_kernel(tc, x, w_q, w_k, w_v, out_0, out_1, out_2):
         root(PAIR, PAIR)
         scale(0, PAIR)
         turn(0)
+        warm_up(2)
         group_weight(0, on_vector)
         scale(PAIR, PAIR)
         turn(1)
+        warm_up(2)
         sums(GROUP, GROUP)
         group(0, on_scalar)
         square(4)

@@ -22,6 +22,7 @@ GROUP = 4
 GROUPS = TILES // GROUP
 COLUMNS = 4 * 128
 PROJECTIONS = 3
+MERGED = [[], [(6, 7)], [(4, 5), (6, 7)]]
 
 FLOPS = 2 * TOKENS * FEATURES * COLUMNS * PROJECTIONS
 
@@ -41,7 +42,8 @@ def tile_encoder_pa_t_kernel(tc, x, w_q, w_k, w_v, out_0, out_1, out_2):
         square_pool = ctx.enter_context(tc.tile_pool(name="square", bufs=4))
         xn_pool = ctx.enter_context(tc.tile_pool(name="xn", bufs=6))
         mx_pool = ctx.enter_context(tc.tile_pool(name="mx", bufs=6))
-        result_pool = ctx.enter_context(tc.tile_pool(name="result", bufs=4))
+        result_pool = ctx.enter_context(tc.tile_pool(name="result", bufs=3))
+        double_pool = ctx.enter_context(tc.tile_pool(name="double", bufs=2))
         turned_pool = ctx.enter_context(tc.psum_pool(name="turned", bufs=2))
         product_pool = ctx.enter_context(tc.psum_pool(name="product", bufs=6))
 
@@ -196,20 +198,74 @@ def tile_encoder_pa_t_kernel(tc, x, w_q, w_k, w_v, out_0, out_1, out_2):
                 stop=True,
             )
 
+        def store_of(tile, i):
+            g = tile // GROUP
+            for pair in MERGED[i]:
+                if g in pair:
+                    return pair[0] * GROUP, 2 * GROUP
+            return g * GROUP, GROUP
+
         def empty(tile, i, copy):
-            g, j = divmod(tile, GROUP)
-            if j == 0:
-                results[i] = result_pool.tile(
-                    [P, GROUP, COLUMNS], F32, tag="result%d" % i, name="result"
+            first, count = store_of(tile, i)
+            if tile == first:
+                pool = double_pool if count > GROUP else result_pool
+                results[i] = pool.tile(
+                    [P, count, COLUMNS], F32, tag="result%d" % i, name="result"
                 )
-            copy(out=results[i][:, j, :], in_=products[tile, i][:])
-            if j == GROUP - 1:
+            copy(out=results[i][:, tile - first, :], in_=products[tile, i][:])
+            if tile == first + count - 1:
                 nc.sync.dma_start(
-                    out=out_tiles[i][:, g * GROUP : (g + 1) * GROUP, :], in_=results[i][:]
+                    out=out_tiles[i][:, first : first + count, :], in_=results[i][:]
                 )
 
         on_scalar = nc.scalar.copy
         on_vector = nc.vector.tensor_copy
+
+        def steady_step(g):
+            a = g * GROUP
+            b = a + GROUP
+            c = b + GROUP
+            pairs = [b // PAIR, b // PAIR + 1] if b < TILES else []
+            squares_of = [c, c + 1, c + 2, c + 3] if c < TILES else []
+            if squares_of:
+                sums(c, GROUP)
+            if pairs:
+                scale(b, GROUP)
+            for i in (0, 1):
+                for j in range(GROUP):
+                    project(a + j, i)
+            for pair in pairs:
+                turn(pair)
+            empty(a, 0, on_scalar)
+            empty(a + 1, 0, on_vector)
+            for tile in squares_of[:1]:
+                square(tile)
+            empty(a + 2, 0, on_scalar)
+            empty(a + 3, 0, on_vector)
+            for tile in squares_of[1:2]:
+                square(tile)
+            empty(a, 1, on_scalar)
+            empty(a + 1, 1, on_vector)
+            for j in range(GROUP):
+                project(a + j, 2)
+            for tile in squares_of[2:3]:
+                square(tile)
+            empty(a + 2, 1, on_scalar)
+            empty(a + 3, 1, on_vector)
+            for tile in squares_of[3:]:
+                square(tile)
+            for pair in pairs:
+                group(pair, on_vector)
+            for pair in pairs[:1]:
+                quantise(pair)
+            empty(a, 2, on_scalar)
+            if squares_of:
+                root(c, GROUP)
+            empty(a + 1, 2, on_vector)
+            for pair in pairs[1:]:
+                quantise(pair)
+            empty(a + 2, 2, on_scalar)
+            empty(a + 3, 2, on_vector)
 
         def step(g, now, ahead):
             a = g * GROUP
@@ -324,9 +380,7 @@ def tile_encoder_pa_t_kernel(tc, x, w_q, w_k, w_v, out_0, out_1, out_2):
         empty(2, 2, on_scalar)
         empty(3, 2, on_scalar)
         step(1, [10], [12,13,14])
-        step(2, [15], [16,17,18,19])
-        step(3, [], [20,21,22,23])
-        step(4, [], [24,25,26,27])
-        step(5, [], [28,29,30,31])
-        step(6, [], [])
-        step(7, [], [])
+        square(15)
+        root(12, GROUP)
+        for g in range(2, GROUPS):
+            steady_step(g)

from contextlib import ExitStack

import concourse.mybir as mybir
from concourse.masks import make_identity

BF16 = mybir.dt.bfloat16
F32 = mybir.dt.float32
U32 = mybir.dt.uint32
U8 = mybir.dt.uint8
FP8X4 = mybir.dt.float8_e4m3fn_x4
ACT = mybir.ActivationFunctionType
ALU = mybir.AluOpType

P = 128
PACK = 4
FEATURES = P * PACK
HALVES = 2
TOKENS = 4 * 1024
TILES = TOKENS // P
PAIR = 2
GROUP = 4
GROUPS = TILES // GROUP
COLUMNS = 4 * 128
PROJECTIONS = 3
MERGED = [[], [(6, 7)], [(4, 5), (6, 7)]]

FLOPS = 2 * TOKENS * FEATURES * COLUMNS * PROJECTIONS


def tile_encoder_pa_t_kernel(tc, x, w_q, w_k, w_v, out_0, out_1, out_2):
    nc = tc.nc
    x_tiles = x.rearrange("b (q j) e -> (b q) j e", j=TILES)
    out_tiles = [
        out.rearrange("b (q j) h d -> (b q) j (h d)", j=TILES)
        for out in (out_0, out_1, out_2)
    ]

    with ExitStack() as ctx:
        keep = ctx.enter_context(tc.tile_pool(name="keep", bufs=1))
        w_pool = ctx.enter_context(tc.tile_pool(name="w", bufs=PROJECTIONS))
        stat_pool = ctx.enter_context(tc.tile_pool(name="stat", bufs=4))
        square_pool = ctx.enter_context(tc.tile_pool(name="square", bufs=4))
        xn_pool = ctx.enter_context(tc.tile_pool(name="xn", bufs=6))
        mx_pool = ctx.enter_context(tc.tile_pool(name="mx", bufs=6))
        result_pool = ctx.enter_context(tc.tile_pool(name="result", bufs=3))
        double_pool = ctx.enter_context(tc.tile_pool(name="double", bufs=2))
        turned_pool = ctx.enter_context(tc.psum_pool(name="turned", bufs=2))
        product_pool = ctx.enter_context(tc.psum_pool(name="product", bufs=6))

        identity = keep.tile([P, P], F32)
        make_identity(nc, identity[:])

        ctx.enter_context(tc.manual_schedule())

        one = keep.tile([P, 1], F32)
        nc.vector.memset(one[:], 1.0)
        root_of_one = keep.tile([P, 1], F32)
        nc.scalar.activation(out=root_of_one[:], in_=one[:], func=ACT.Abs_reciprocal_sqrt)

        x_all = keep.tile([P, TILES, FEATURES], BF16)
        w_raws = []

        def load_x(first, count):
            tiles = slice(first, first + count)
            nc.sync.dma_start(out=x_all[:, tiles, :], in_=x_tiles[:, tiles, :])

        def load_weight(w):
            w_raw = w_pool.tile([P, PACK, COLUMNS], BF16)
            nc.sync.dma_start(
                out=w_raw[:].rearrange("p t n -> p (t n)"),
                in_=w.rearrange("(p t) h d -> p (t h d)", t=PACK),
            )
            w_raws.append(w_raw)

        load_x(0, PAIR)
        load_x(PAIR, PAIR)
        load_weight(w_q)
        load_x(GROUP, GROUP)
        load_weight(w_k)
        load_weight(w_v)
        load_x(2 * GROUP, 2 * GROUP)
        load_x(4 * GROUP, 4 * GROUP)

        zeros = keep.tile([P, COLUMNS], BF16)
        nc.vector.memset(zeros[:], 0.0)
        warm = product_pool.tile([P, COLUMNS], F32, name="product")

        def warm_up(count):
            for _ in range(count):
                nc.tensor.matmul(out=warm[:], lhsT=zeros[:, :P], rhs=zeros[:], start=True, stop=True)

        w_grouped = {}
        w_codes = {}
        w_scales = {}

        def group_weight(i, copy):
            w_grouped[i] = w_pool.tile([P, COLUMNS, PACK], BF16, align_bytes=64, name="w_grouped")
            copy(out=w_grouped[i][:], in_=w_raws[i][:].rearrange("p t n -> p n t"))

        def quantise_weight(i):
            w_codes[i] = w_pool.tile([P, COLUMNS], U32, align_bytes=64, name="w_codes")
            w_scales[i] = w_pool.tile([P, COLUMNS], U8, align_bytes=64, name="w_scales")
            nc.vector.quantize_mx(
                out=w_codes[i][:].bitcast(FP8X4),
                scales=w_scales[i][:],
                in_=w_grouped[i][:].rearrange("p n t -> p (n t)"),
            )

        sum_squares = {}
        inverse_rms = {}
        xn = {}
        turned = {}
        grouped = {}
        codes = {}
        scales = {}

        def sums(first, count):
            block = stat_pool.tile([P, GROUP], F32, name="sum_squares")
            for j in range(count):
                sum_squares[first + j] = block[:, j : j + 1]
            inverse_rms[first] = block[:, :count]

        def square(tile):
            squares = square_pool.tile([P, FEATURES], BF16)
            nc.scalar.activation(
                out=squares[:], in_=x_all[:, tile, :], func=ACT.Square, accum_out=sum_squares[tile]
            )

        def square_on_vector(tile):
            squares = square_pool.tile([P, FEATURES], BF16)
            nc.vector.scalar_tensor_tensor(
                out=squares[:],
                in0=x_all[:, tile, :],
                scalar=1.0,
                in1=x_all[:, tile, :],
                op0=ALU.mult,
                op1=ALU.mult,
                accum_out=sum_squares[tile],
            )

        def root(first, count):
            roots = stat_pool.tile([P, GROUP], F32, name="inverse_rms")
            nc.scalar.activation(
                out=roots[:, :count],
                in_=inverse_rms[first],
                func=ACT.Abs_reciprocal_sqrt,
                scale=1.0 / FEATURES,
            )
            inverse_rms[first] = roots[:, :count]

        def scale(first, count):
            for j in range(count):
                if j % PAIR == 0:
                    pair_xn = xn_pool.tile([P, PAIR, FEATURES], BF16)
                xn[first + j] = pair_xn[:, j % PAIR, :]
                nc.vector.tensor_scalar_mul(
                    out=xn[first + j],
                    in0=x_all[:, first + j, :],
                    scalar1=inverse_rms[first][:, j : j + 1],
                )

        def turn(pair):
            turned[pair] = turned_pool.tile([P, PAIR, HALVES, P], F32, name="turned")
            for j in range(PAIR):
                words = xn[pair * PAIR + j].bitcast(F32)
                for u in range(HALVES):
                    nc.tensor.transpose(turned[pair][:, j, u, :], words[:, u::HALVES], identity[:])

        def group(pair, copy):
            grouped[pair] = mx_pool.tile([P, PAIR, P, PACK], BF16, align_bytes=64, name="grouped")
            copy(
                out=grouped[pair][:].bitcast(F32), in_=turned[pair][:].rearrange("p j u r -> p j r u")
            )

        def quantise(pair):
            codes[pair] = mx_pool.tile([P, PAIR * P], U32, align_bytes=64, name="codes")
            scales[pair] = mx_pool.tile([P, PAIR * P], U8, align_bytes=64, name="scales")
            nc.vector.quantize_mx(
                out=codes[pair][:].bitcast(FP8X4),
                scales=scales[pair][:],
                in_=grouped[pair][:].rearrange("p j r t -> p (j r t)"),
            )

        products = {}
        results = {}

        def project(tile, i):
            pair, j = divmod(tile, PAIR)
            tokens = slice(j * P, (j + 1) * P)
            products[tile, i] = product_pool.tile([P, COLUMNS], F32, name="product")
            nc.tensor.matmul_mx(
                out=products[tile, i][:],
                lhsT=codes[pair][:, tokens].bitcast(FP8X4),
                lhsT_scale=scales[pair][:, tokens],
                rhs=w_codes[i][:].bitcast(FP8X4),
                rhs_scale=w_scales[i][:],
                start=True,
                stop=True,
            )

        def store_of(tile, i):
            g = tile // GROUP
            for pair in MERGED[i]:
                if g in pair:
                    return pair[0] * GROUP, 2 * GROUP
            return g * GROUP, GROUP

        def empty(tile, i, copy):
            first, count = store_of(tile, i)
            if tile == first:
                pool = double_pool if count > GROUP else result_pool
                results[i] = pool.tile(
                    [P, count, COLUMNS], F32, tag="result%d" % i, name="result"
                )
            copy(out=results[i][:, tile - first, :], in_=products[tile, i][:])
            if tile == first + count - 1:
                nc.sync.dma_start(
                    out=out_tiles[i][:, first : first + count, :], in_=results[i][:]
                )

        on_scalar = nc.scalar.copy
        on_vector = nc.vector.tensor_copy

        def steady_step(g):
            a = g * GROUP
            b = a + GROUP
            c = b + GROUP
            pairs = [b // PAIR, b // PAIR + 1] if b < TILES else []
            squares_of = [c, c + 1, c + 2, c + 3] if c < TILES else []
            if squares_of:
                sums(c, GROUP)
            if pairs:
                scale(b, GROUP)
            for i in (0, 1):
                for j in range(GROUP):
                    project(a + j, i)
            for pair in pairs:
                turn(pair)
            empty(a, 0, on_scalar)
            empty(a + 1, 0, on_vector)
            for tile in squares_of[:1]:
                square(tile)
            empty(a + 2, 0, on_scalar)
            empty(a + 3, 0, on_vector)
            for tile in squares_of[1:2]:
                square(tile)
            empty(a, 1, on_scalar)
            empty(a + 1, 1, on_vector)
            for j in range(GROUP):
                project(a + j, 2)
            for tile in squares_of[2:3]:
                square(tile)
            empty(a + 2, 1, on_scalar)
            empty(a + 3, 1, on_vector)
            for tile in squares_of[3:]:
                square(tile)
            for pair in pairs:
                group(pair, on_vector)
            for pair in pairs[:1]:
                quantise(pair)
            empty(a, 2, on_scalar)
            if squares_of:
                root(c, GROUP)
            empty(a + 1, 2, on_vector)
            for pair in pairs[1:]:
                quantise(pair)
            empty(a + 2, 2, on_scalar)
            empty(a + 3, 2, on_vector)

        def step(g, now, ahead):
            a = g * GROUP
            b = a + GROUP
            pairs = [b // PAIR, b // PAIR + 1]
            more = g + 1 < GROUPS
            if ahead and ahead[0] == b + GROUP:
                sums(b + GROUP, GROUP)
            now = list(now)
            ahead = list(ahead)
            for i in (0, 1):
                for j in range(GROUP):
                    project(a + j, i)
            empty(a, 0, on_scalar)
            empty(a + 1, 0, on_vector)
            for tile in now[:1]:
                square(tile)
            empty(a + 2, 0, on_scalar)
            empty(a + 3, 0, on_vector)
            for tile in now[1:]:
                square(tile)
            if now:
                root(b, GROUP)
            empty(a, 1, on_scalar)
            empty(a + 1, 1, on_vector)
            if more:
                scale(b, GROUP)
                for pair in pairs:
                    turn(pair)
            for j in range(GROUP):
                project(a + j, 2)
            empty(a + 2, 1, on_scalar)
            empty(a + 3, 1, on_vector)
            for tile in ahead[:2]:
                square(tile)
            if more:
                group(pairs[0], on_vector)
                group(pairs[1], on_vector)
                quantise(pairs[0])
            empty(a, 2, on_scalar)
            empty(a + 1, 2, on_vector)
            for tile in ahead[2:3]:
                square(tile)
            if more:
                quantise(pairs[1])
            empty(a + 2, 2, on_scalar)
            empty(a + 3, 2, on_vector)
            for tile in ahead[3:]:
                square(tile)
            if len(ahead) > 0 and ahead[-1] == b + 2 * GROUP - 1:
                root(b + GROUP, GROUP)


        warm_up(6)
        sums(0, PAIR)
        square(0)
        square_on_vector(1)
        root(0, PAIR)
        sums(PAIR, PAIR)
        square(2)
        square_on_vector(3)
        root(PAIR, PAIR)
        scale(0, PAIR)
        turn(0)
        warm_up(2)
        group_weight(0, on_vector)
        scale(PAIR, PAIR)
        turn(1)
        warm_up(2)
        sums(GROUP, GROUP)
        group(0, on_scalar)
        square(4)
        quantise_weight(0)
        quantise(0)
        group(1, on_scalar)
        group_weight(1, on_vector)
        quantise(1)
        for j in range(GROUP):
            project(j, 0)
        square(5)
        quantise_weight(1)
        empty(0, 0, on_scalar)
        empty(1, 0, on_vector)
        square(6)
        empty(2, 0, on_scalar)
        empty(3, 0, on_vector)
        square(7)
        root(GROUP, GROUP)
        for j in range(GROUP):
            project(j, 1)
        group_weight(2, on_vector)
        empty(0, 1, on_scalar)
        scale(GROUP, GROUP)
        turn(2)
        turn(3)
        empty(1, 1, on_scalar)
        empty(2, 1, on_scalar)
        quantise_weight(2)
        empty(3, 1, on_vector)
        for j in range(GROUP):
            project(j, 2)
        sums(8, GROUP)
        square(8)
        square(9)
        group(2, on_vector)
        group(3, on_vector)
        quantise(2)
        empty(0, 2, on_scalar)
        empty(1, 2, on_vector)
        quantise(3)
        square_on_vector(11)
        empty(2, 2, on_scalar)
        empty(3, 2, on_scalar)
        step(1, [10], [12,13,14])
        square(15)
        root(12, GROUP)
        for g in range(2, GROUPS):
            steady_step(g)
